import numpy as np
import ml_dtypes


def mxq(x, axis, fmt="e4m3"):
    dtype, down = {"e4m3": (ml_dtypes.float8_e4m3fn, 7), "e5m2": (ml_dtypes.float8_e5m2, 14)}[fmt]
    v = np.moveaxis(np.asarray(x, np.float32).astype(ml_dtypes.bfloat16).astype(np.float64), axis, -1)
    blocks = v.reshape(v.shape[:-1] + (-1, 32))
    amax = np.abs(blocks).max(-1, keepdims=True)
    byte = np.maximum(np.where(amax > 0, np.frexp(amax)[1] - 1 + 127, 0) - down, 1)
    scale = np.exp2(byte - 127.0)
    codes = (blocks / scale).astype(np.float32).astype(dtype).astype(np.float64)
    return np.moveaxis((codes * scale).reshape(v.shape), -1, axis)


WIDE = False


def mx_kscale(k):
    if not WIDE:
        return np.ones(k)
    levels = np.array([10, -10, 5, -5, 0])
    a = np.random.permutation(np.resize(levels, k // 512 * 4)).reshape(k // 512, 4)
    idx = np.arange(k)
    return np.exp2(a[idx // 512, idx % 128 // 32])


BF16 = ml_dtypes.bfloat16


def bf(x):
    return np.asarray(x, np.float32).astype(BF16)


def f64(x):
    return np.asarray(x).astype(np.float64)


E2M1 = np.array([0.0, 0.5, 1.0, 1.5, 2.0, 3.0, 4.0, 6.0, -0.0, -0.5, -1.0, -1.5, -2.0, -3.0, -4.0, -6.0])


def pack_weight(w, fmt):
    k, n = w.shape
    w = f64(bf(w)).reshape(k // 32, 32, n)
    amax = np.abs(w).max(1)
    if fmt == "e4m3":
        byte = np.frexp(amax)[1] - 1 + 127 - 7
    else:
        mant, ex = np.frexp(amax / 6.0)
        byte = np.where(mant > 0.5, ex, ex - 1) + 127
    byte = np.clip(np.where(amax > 0, byte, 1), 1, 254)
    scaled = (w * np.exp2(127.0 - byte)[:, None, :]).reshape(k, n).astype(np.float32)
    by_word = np.ascontiguousarray(scaled.reshape(k // 512, 128, 4, n).transpose(0, 1, 3, 2))
    if fmt == "e4m3":
        words = by_word.astype(ml_dtypes.float8_e4m3fn).view(np.uint8)
    else:
        c = by_word.astype(ml_dtypes.float4_e2m1fn).view(np.uint8) & 0xF
        words = c[..., 0::2] | (c[..., 1::2] << 4)
    return np.ascontiguousarray(words), np.ascontiguousarray(byte.astype(np.uint8).reshape(k // 512, 16, n))


def unpack_weight(words, scales, fmt):
    g, p, n, _ = words.shape
    if fmt == "e4m3":
        vals = np.ascontiguousarray(words).view(ml_dtypes.float8_e4m3fn).astype(np.float64)
    else:
        nib = np.empty((g, p, n, 4), np.uint8)
        nib[..., 0::2] = words & 0xF
        nib[..., 1::2] = words >> 4
        vals = E2M1[nib]
    vals = vals * np.repeat(np.exp2(scales.astype(np.float64) - 127.0), 8, axis=1)[..., None]
    return vals.transpose(0, 1, 3, 2).reshape(g * 512, n)


B, C, HH, WW = 4, 512, 32, 32
P = HH * WW
EPS = 1e-05
FMT = "e4m3"


def setup_inputs():
    s = mx_kscale(C)
    lev = np.random.uniform(0.5, 1.5, (B, C, 1, 1))
    x = (lev + 0.8 * np.random.standard_normal((B, C, HH, WW))) * s[None, :, None, None]
    r = s[:, None] / s[None, :]
    Wc = np.random.standard_normal((C, C)) * 0.7 / np.sqrt(C) * r
    bc = bf(np.random.standard_normal(C) * 0.3 * s)
    W1 = np.random.standard_normal((C, C)) * 1.4 / np.sqrt(C) * r
    b1 = bf(np.random.standard_normal(C) * 0.5 * s)
    Wc_words, Wc_scales = pack_weight(np.ascontiguousarray(Wc.T), FMT)
    W1_words, W1_scales = pack_weight(np.ascontiguousarray(W1.T), FMT)
    return {"x": bf(x),
            "Wc_words": Wc_words, "Wc_scales": Wc_scales, "bc": bc,
            "W1_words": W1_words, "W1_scales": W1_scales, "b1": b1}


def reference(x, Wc_words, Wc_scales, bc, W1_words, W1_scales, b1):
    x = f64(x)
    out1 = x.mean(axis=(2, 3), keepdims=True)
    out3 = x.max(axis=(2, 3), keepdims=True)
    xq = mxq(x, 1, "e4m3").reshape(B, C, P)
    out2 = ((unpack_weight(Wc_words, Wc_scales, FMT).T @ xq) + f64(bc)[None, :, None]).reshape(B, C, HH, WW)
    out4 = ((unpack_weight(W1_words, W1_scales, FMT).T @ xq) + f64(b1)[None, :, None]).reshape(B, C, HH, WW)
    return out2 / (out1 + EPS), out4 / (out3 + EPS)

@@ -1,0 +1,249 @@
+from contextlib import ExitStack
+
+import concourse.mybir as mybir
+from concourse.masks import make_identity
+
+F32 = mybir.dt.float32
+BF16 = mybir.dt.bfloat16
+I32 = mybir.dt.int32
+U32 = mybir.dt.uint32
+U8 = mybir.dt.uint8
+FP8X4 = mybir.dt.float8_e4m3fn_x4
+ALU = mybir.AluOpType
+IDENTITY = mybir.ActivationFunctionType.Identity
+AXIS_X = mybir.AxisListType.X
+
+P = 128
+PACK = 4
+QUADRANT = 32
+IMAGES = 4
+CHANNELS = P * PACK
+PIXELS = 1024
+ROW_TILES = CHANNELS // P
+N_PASS = 512
+HALVES = PIXELS // N_PASS
+RESULTS = 2
+EPS = 1e-5
+RUN = 4
+TREE_END = 64
+
+FLOPS = 2 * RESULTS * IMAGES * CHANNELS * CHANNELS * PIXELS
+
+
+def tile_wb_pa_t_kernel(tc, x, Wc_words, Wc_scales, bc, W1_words, W1_scales, b1, out_0, out_1):
+    nc = tc.nc
+    words_in = (Wc_words, W1_words)
+    scales_in = (Wc_scales, W1_scales)
+    bias_in = (bc, b1)
+    outs = (out_0, out_1)
+
+    with ExitStack() as ctx:
+        consts = ctx.enter_context(tc.tile_pool(name="consts", bufs=1))
+        images = ctx.enter_context(tc.tile_pool(name="images", bufs=IMAGES))
+        work = ctx.enter_context(tc.tile_pool(name="work", bufs=2))
+        small = ctx.enter_context(tc.tile_pool(name="small", bufs=2))
+        results = ctx.enter_context(tc.tile_pool(name="results", bufs=16))
+        banks = ctx.enter_context(tc.psum_pool(name="banks", bufs=6))
+        moves = ctx.enter_context(tc.psum_pool(name="moves", bufs=1))
+        ctx.enter_context(tc.manual_schedule())
+
+        bias4 = []
+        for r in range(RESULTS):
+            bias_r = consts.tile([P, PACK], BF16, name="bias4_%d" % r)
+            nc.scalar.dma_start(out=bias_r[:], in_=bias_in[r].rearrange("(p j) -> p j", j=PACK))
+            bias4.append(bias_r)
+
+        w_words = consts.tile([P, RESULTS, CHANNELS], U32, align_bytes=64)
+        w_scales = consts.tile([P, RESULTS, CHANNELS], U8, align_bytes=64)
+        nc.vector.memset(w_scales[:].bitcast(I32), 0)
+
+        def load_image(b):
+            raw = images.tile([P, PACK, PIXELS], BF16, name="raw")
+            nc.sync.dma_start(out=raw[:], in_=x[b].rearrange("(p j) h w -> p j (h w)", j=PACK))
+            return raw
+
+        def load_scales(r):
+            for q in range(P // QUADRANT):
+                nc.sync.dma_start(
+                    out=w_scales[QUADRANT * q : QUADRANT * q + PACK, r, :].bitcast(I32),
+                    in_=scales_in[r][0, PACK * q : PACK * q + PACK, :].bitcast(I32),
+                )
+
+        def load_words(r):
+            nc.sync.dma_start(
+                out=w_words[:, r, :].bitcast(I32),
+                in_=words_in[r][0].rearrange("p n t -> p (n t)").bitcast(I32),
+            )
+
+        raws = [load_image(0)]
+        load_scales(0)
+        load_words(0)
+        raws.append(load_image(1))
+        load_words(1)
+        load_scales(1)
+        raws.append(load_image(2))
+        raws.append(load_image(3))
+
+        ident = consts.tile([P, P], F32)
+        make_identity(nc, ident[:])
+        quad = consts.tile([P, ROW_TILES], F32)
+        nc.vector.tensor_reduce(
+            out=quad[:], in_=ident[:].rearrange("p (t l) -> p t l", l=QUADRANT), axis=AXIS_X, op=ALU.add
+        )
+        lane = consts.tile([P, QUADRANT], F32)
+        nc.vector.tensor_reduce(
+            out=lane[:], in_=ident[:].rearrange("p (t l) -> p l t", l=QUADRANT), axis=AXIS_X, op=ALU.add
+        )
+        quad_mean = consts.tile([P, ROW_TILES], F32)
+        nc.vector.tensor_scalar_mul(out=quad_mean[:], in0=quad[:], scalar1=1.0 / PIXELS)
+        fold = consts.tile([P, PACK, QUADRANT, PACK], F32)
+        nc.vector.memset(fold[:], 0.0)
+        for j in range(PACK):
+            nc.vector.tensor_copy(out=fold[:, j, :, j], in_=lane[:])
+
+        def over_tiles(vec4):
+            return vec4[:].unsqueeze(2).to_broadcast([P, PACK, ROW_TILES])
+
+        def over_pack(mask):
+            return mask[:].unsqueeze(1).to_broadcast([P, PACK, ROW_TILES])
+
+        def move_to_rows(spread, name):
+            moved = moves.tile([P, ROW_TILES, RESULTS], F32, name=name)
+            for j in range(PACK):
+                nc.tensor.matmul(
+                    out=moved[:].rearrange("p t r -> p (t r)"),
+                    lhsT=fold[:, j, :, :].rearrange("p l i -> p (l i)"),
+                    rhs=spread[:, j, :, :].rearrange("p t r -> p (t r)"),
+                    start=(j == 0),
+                    stop=(j == PACK - 1),
+                )
+            return moved
+
+        bias_spread = consts.tile([P, PACK, ROW_TILES, RESULTS], F32)
+        for r in range(RESULTS):
+            nc.vector.tensor_tensor(
+                out=bias_spread[:, :, :, r], in0=over_tiles(bias4[r]), in1=over_pack(quad), op=ALU.mult
+            )
+        bias_rows = move_to_rows(bias_spread, "bias_rows")
+
+        def prepare(b):
+            raw = raws[b]
+            sum4 = small.tile([P, PACK], F32, name="sum4")
+            max4 = small.tile([P, PACK], F32, name="max4")
+            top = work.tile([P, PACK, PIXELS // 2], BF16, name="top")
+            if b == 0:
+                waste = consts.tile([P, PACK, PIXELS], BF16, name="waste_scalar")
+            else:
+                waste = work.tile([P, PACK, PIXELS // 2], F32, name="waste_vector")
+            width = PIXELS
+            source = raw
+            for j in range(PACK):
+                width //= 2
+                nc.vector.tensor_max(
+                    out=top[:, :, :width], in0=source[:, :, :width], in1=source[:, :, width : 2 * width]
+                )
+                source = top
+                if b == 0:
+                    nc.scalar.activation(
+                        out=waste[:, j, :], in_=raw[:, j, :], func=IDENTITY, accum_out=sum4[:, j : j + 1]
+                    )
+                else:
+                    nc.vector.scalar_tensor_tensor(
+                        out=waste[:, j, :],
+                        in0=raw[:, j, : PIXELS // 2],
+                        scalar=1.0,
+                        in1=raw[:, j, PIXELS // 2 :],
+                        op0=ALU.mult,
+                        op1=ALU.add,
+                        accum_out=sum4[:, j : j + 1],
+                    )
+            assert width == TREE_END
+            nc.vector.tensor_reduce(out=max4[:], in_=top[:, :, :width], axis=AXIS_X, op=ALU.max)
+
+            grouped = work.tile([P, PIXELS, PACK], BF16, align_bytes=64, name="grouped")
+            codes = work.tile([P, PIXELS], U32, align_bytes=64, name="codes")
+            scales = work.tile([P, PIXELS], U8, align_bytes=64, name="scales")
+            spread = small.tile([P, PACK, ROW_TILES, RESULTS], F32, name="spread")
+
+            def regroup(h):
+                cols = slice(h * N_PASS, (h + 1) * N_PASS)
+                nc.vector.tensor_copy(
+                    out=grouped[:, cols, :].rearrange("p (c i) j -> p c j i", i=RUN),
+                    in_=raw[:, :, cols].rearrange("p j (c i) -> p c j i", i=RUN),
+                )
+
+            regroup(0)
+            nc.vector.scalar_tensor_tensor(
+                out=spread[:, :, :, 0],
+                in0=over_tiles(sum4),
+                scalar=PIXELS * EPS,
+                in1=over_pack(quad_mean),
+                op0=ALU.add,
+                op1=ALU.mult,
+            )
+            nc.vector.scalar_tensor_tensor(
+                out=spread[:, :, :, 1],
+                in0=over_tiles(max4),
+                scalar=EPS,
+                in1=over_pack(quad),
+                op0=ALU.add,
+                op1=ALU.mult,
+            )
+            divisors = move_to_rows(spread, "divisors")
+            regroup(1)
+            for h in range(HALVES):
+                cols = slice(h * N_PASS, (h + 1) * N_PASS)
+                nc.vector.quantize_mx(
+                    out=codes[:, cols].bitcast(FP8X4),
+                    scales=scales[:, cols],
+                    in_=grouped[:, cols, :].rearrange("p w j -> p (w j)"),
+                )
+            gain = small.tile([P, ROW_TILES, RESULTS], F32, name="gain")
+            nc.vector.reciprocal(out=gain[:], in_=divisors[:])
+            shift = small.tile([P, ROW_TILES, RESULTS], F32, name="shift")
+            nc.vector.tensor_mul(out=shift[:], in0=bias_rows[:], in1=gain[:])
+            return codes, scales, gain, shift
+
+        def multiply(b, prepared):
+            codes, scales, gain, shift = prepared
+            for r in range(RESULTS):
+                for t in range(ROW_TILES):
+                    rows = slice(t * P, (t + 1) * P)
+                    on_vector = b == IMAGES - 1 and t % 2 == 1
+                    done = results.tile([P, PIXELS], F32, name="done")
+                    for h in range(HALVES):
+                        cols = slice(h * N_PASS, (h + 1) * N_PASS)
+                        acc = banks.tile([P, N_PASS], F32, name="acc")
+                        nc.tensor.matmul_mx(
+                            out=acc[:],
+                            lhsT=w_words[:, r, rows].bitcast(FP8X4),
+                            lhsT_scale=w_scales[:, r, rows],
+                            rhs=codes[:, cols].bitcast(FP8X4),
+                            rhs_scale=scales[:, cols],
+                            start=True,
+                            stop=True,
+                        )
+                        if on_vector:
+                            nc.vector.tensor_scalar(
+                                out=done[:, cols],
+                                in0=acc[:],
+                                scalar1=gain[:, t, r : r + 1],
+                                scalar2=shift[:, t, r : r + 1],
+                                op0=ALU.mult,
+                                op1=ALU.add,
+                            )
+                        else:
+                            nc.scalar.activation(
+                                out=done[:, cols],
+                                in_=acc[:],
+                                func=IDENTITY,
+                                bias=shift[:, t, r : r + 1],
+                                scale=gain[:, t, r : r + 1],
+                            )
+                    nc.sync.dma_start(out=outs[r][b, rows].rearrange("c h w -> c (h w)"), in_=done[:])
+
+        prepared = prepare(0)
+        for b in range(IMAGES):
+            multiply(b, prepared)
+            if b + 1 < IMAGES:
+                prepared = prepare(b + 1)

@@ -25,7 +25,7 @@ HALVES = PIXELS // N_PASS
 RESULTS = 2
 EPS = 1e-5
 RUN = 4
-TREE_END = 64
+STEPS = 4
 
 FLOPS = 2 * RESULTS * IMAGES * CHANNELS * CHANNELS * PIXELS
 
@@ -135,9 +135,14 @@ def tile_wb_pa_t_kernel(tc, x, Wc_words, Wc_scales, bc, W1_words, W1_scales, b1,
                 waste = consts.tile([P, PACK, PIXELS], BF16, name="waste_scalar")
             else:
                 waste = work.tile([P, PACK, PIXELS // 2], F32, name="waste_vector")
+            grouped = work.tile([P, PIXELS, PACK], BF16, align_bytes=64, name="grouped")
+            codes = work.tile([P, PIXELS], U32, align_bytes=64, name="codes")
+            scales = work.tile([P, PIXELS], U8, align_bytes=64, name="scales")
+            spread = small.tile([P, PACK, ROW_TILES, RESULTS], F32, name="spread")
+
             width = PIXELS
             source = raw
-            for j in range(PACK):
+            for j in range(STEPS):
                 width //= 2
                 nc.vector.tensor_max(
                     out=top[:, :, :width], in0=source[:, :, :width], in1=source[:, :, width : 2 * width]
@@ -157,22 +162,13 @@ def tile_wb_pa_t_kernel(tc, x, Wc_words, Wc_scales, bc, W1_words, W1_scales, b1,
                         op1=ALU.add,
                         accum_out=sum4[:, j : j + 1],
                     )
-            assert width == TREE_END
-            nc.vector.tensor_reduce(out=max4[:], in_=top[:, :, :width], axis=AXIS_X, op=ALU.max)
-
-            grouped = work.tile([P, PIXELS, PACK], BF16, align_bytes=64, name="grouped")
-            codes = work.tile([P, PIXELS], U32, align_bytes=64, name="codes")
-            scales = work.tile([P, PIXELS], U8, align_bytes=64, name="scales")
-            spread = small.tile([P, PACK, ROW_TILES, RESULTS], F32, name="spread")
-
-            def regroup(h):
-                cols = slice(h * N_PASS, (h + 1) * N_PASS)
+                cols = slice(j * PIXELS // STEPS, (j + 1) * PIXELS // STEPS)
                 nc.vector.tensor_copy(
                     out=grouped[:, cols, :].rearrange("p (c i) j -> p c j i", i=RUN),
                     in_=raw[:, :, cols].rearrange("p j (c i) -> p c j i", i=RUN),
                 )
+            nc.vector.tensor_reduce(out=max4[:], in_=top[:, :, :width], axis=AXIS_X, op=ALU.max)
 
-            regroup(0)
             nc.vector.scalar_tensor_tensor(
                 out=spread[:, :, :, 0],
                 in0=over_tiles(sum4),
@@ -190,7 +186,6 @@ def tile_wb_pa_t_kernel(tc, x, Wc_words, Wc_scales, bc, W1_words, W1_scales, b1,
                 op1=ALU.mult,
             )
             divisors = move_to_rows(spread, "divisors")
-            regroup(1)
             for h in range(HALVES):
                 cols = slice(h * N_PASS, (h + 1) * N_PASS)
                 nc.vector.quantize_mx(

@@ -25,7 +25,8 @@ HALVES = PIXELS // N_PASS
 RESULTS = 2
 EPS = 1e-5
 RUN = 4
-STEPS = 4
+TREE_END = 64
+ROW_PAIRS = (slice(0, 2), slice(2, 4))
 
 FLOPS = 2 * RESULTS * IMAGES * CHANNELS * CHANNELS * PIXELS
 
@@ -59,7 +60,9 @@ def tile_wb_pa_t_kernel(tc, x, Wc_words, Wc_scales, bc, W1_words, W1_scales, b1,
 
         def load_image(b):
             raw = images.tile([P, PACK, PIXELS], BF16, name="raw")
-            nc.sync.dma_start(out=raw[:], in_=x[b].rearrange("(p j) h w -> p j (h w)", j=PACK))
+            rows_of_p = x[b].rearrange("(p j) h w -> p j (h w)", j=PACK)
+            for pair in ROW_PAIRS:
+                nc.sync.dma_start(out=raw[:, pair, :], in_=rows_of_p[:, pair, :])
             return raw
 
         def load_scales(r):
@@ -121,7 +124,7 @@ def tile_wb_pa_t_kernel(tc, x, Wc_words, Wc_scales, bc, W1_words, W1_scales, b1,
 
         bias_spread = consts.tile([P, PACK, ROW_TILES, RESULTS], F32)
         for r in range(RESULTS):
-            nc.vector.tensor_tensor(
+            nc.gpsimd.tensor_tensor(
                 out=bias_spread[:, :, :, r], in0=over_tiles(bias4[r]), in1=over_pack(quad), op=ALU.mult
             )
         bias_rows = move_to_rows(bias_spread, "bias_rows")
@@ -135,19 +138,10 @@ def tile_wb_pa_t_kernel(tc, x, Wc_words, Wc_scales, bc, W1_words, W1_scales, b1,
                 waste = consts.tile([P, PACK, PIXELS], BF16, name="waste_scalar")
             else:
                 waste = work.tile([P, PACK, PIXELS // 2], F32, name="waste_vector")
-            grouped = work.tile([P, PIXELS, PACK], BF16, align_bytes=64, name="grouped")
-            codes = work.tile([P, PIXELS], U32, align_bytes=64, name="codes")
-            scales = work.tile([P, PIXELS], U8, align_bytes=64, name="scales")
-            spread = small.tile([P, PACK, ROW_TILES, RESULTS], F32, name="spread")
-
-            width = PIXELS
-            source = raw
-            for j in range(STEPS):
-                width //= 2
-                nc.vector.tensor_max(
-                    out=top[:, :, :width], in0=source[:, :, :width], in1=source[:, :, width : 2 * width]
-                )
-                source = top
+            width = PIXELS // 2
+            for pair in ROW_PAIRS:
+                nc.vector.tensor_max(out=top[:, pair, :], in0=raw[:, pair, :width], in1=raw[:, pair, width:])
+            for j in range(PACK):
                 if b == 0:
                     nc.scalar.activation(
                         out=waste[:, j, :], in_=raw[:, j, :], func=IDENTITY, accum_out=sum4[:, j : j + 1]
@@ -162,13 +156,27 @@ def tile_wb_pa_t_kernel(tc, x, Wc_words, Wc_scales, bc, W1_words, W1_scales, b1,
                         op1=ALU.add,
                         accum_out=sum4[:, j : j + 1],
                     )
-                cols = slice(j * PIXELS // STEPS, (j + 1) * PIXELS // STEPS)
+                if width > TREE_END:
+                    width //= 2
+                    nc.vector.tensor_max(
+                        out=top[:, :, :width], in0=top[:, :, :width], in1=top[:, :, width : 2 * width]
+                    )
+            assert width == TREE_END
+            nc.vector.tensor_reduce(out=max4[:], in_=top[:, :, :width], axis=AXIS_X, op=ALU.max)
+
+            grouped = work.tile([P, PIXELS, PACK], BF16, align_bytes=64, name="grouped")
+            codes = work.tile([P, PIXELS], U32, align_bytes=64, name="codes")
+            scales = work.tile([P, PIXELS], U8, align_bytes=64, name="scales")
+            spread = small.tile([P, PACK, ROW_TILES, RESULTS], F32, name="spread")
+
+            def regroup(h):
+                cols = slice(h * N_PASS, (h + 1) * N_PASS)
                 nc.vector.tensor_copy(
                     out=grouped[:, cols, :].rearrange("p (c i) j -> p c j i", i=RUN),
                     in_=raw[:, :, cols].rearrange("p j (c i) -> p c j i", i=RUN),
                 )
-            nc.vector.tensor_reduce(out=max4[:], in_=top[:, :, :width], axis=AXIS_X, op=ALU.max)
 
+            regroup(0)
             nc.vector.scalar_tensor_tensor(
                 out=spread[:, :, :, 0],
                 in0=over_tiles(sum4),
@@ -186,6 +194,7 @@ def tile_wb_pa_t_kernel(tc, x, Wc_words, Wc_scales, bc, W1_words, W1_scales, b1,
                 op1=ALU.mult,
             )
             divisors = move_to_rows(spread, "divisors")
+            regroup(1)
             for h in range(HALVES):
                 cols = slice(h * N_PASS, (h + 1) * N_PASS)
                 nc.vector.quantize_mx(

@@ -25,8 +25,12 @@ HALVES = PIXELS // N_PASS
 RESULTS = 2
 EPS = 1e-5
 RUN = 4
-TREE_END = 64
 ROW_PAIRS = (slice(0, 2), slice(2, 4))
+ROWS_ALONE = (slice(0, 1), slice(1, 2), slice(2, 3), slice(3, 4))
+CHUNK = 128
+LEAD = 3
+PASSES = RESULTS * ROW_TILES * HALVES
+EARLY_BANK = 12
 
 FLOPS = 2 * RESULTS * IMAGES * CHANNELS * CHANNELS * PIXELS
 
@@ -54,6 +58,10 @@ def tile_wb_pa_t_kernel(tc, x, Wc_words, Wc_scales, bc, W1_words, W1_scales, b1,
             nc.scalar.dma_start(out=bias_r[:], in_=bias_in[r].rearrange("(p j) -> p j", j=PACK))
             bias4.append(bias_r)
 
+        warm = consts.tile([P, 2], F32)
+        nc.gpsimd.memset(warm[:], 0.0)
+        nc.scalar.activation(out=warm[:, 1:2], in_=warm[:, 0:1], func=IDENTITY)
+
         w_words = consts.tile([P, RESULTS, CHANNELS], U32, align_bytes=64)
         w_scales = consts.tile([P, RESULTS, CHANNELS], U8, align_bytes=64)
         nc.vector.memset(w_scales[:].bitcast(I32), 0)
@@ -61,8 +69,8 @@ def tile_wb_pa_t_kernel(tc, x, Wc_words, Wc_scales, bc, W1_words, W1_scales, b1,
         def load_image(b):
             raw = images.tile([P, PACK, PIXELS], BF16, name="raw")
             rows_of_p = x[b].rearrange("(p j) h w -> p j (h w)", j=PACK)
-            for pair in ROW_PAIRS:
-                nc.sync.dma_start(out=raw[:, pair, :], in_=rows_of_p[:, pair, :])
+            for part_of in ROWS_ALONE if b == 0 else ROW_PAIRS:
+                nc.sync.dma_start(out=raw[:, part_of, :], in_=rows_of_p[:, part_of, :])
             return raw
 
         def load_scales(r):
@@ -89,6 +97,8 @@ def tile_wb_pa_t_kernel(tc, x, Wc_words, Wc_scales, bc, W1_words, W1_scales, b1,
 
         ident = consts.tile([P, P], F32)
         make_identity(nc, ident[:])
+        fold = consts.tile([P, PACK, QUADRANT, PACK], F32)
+        nc.vector.memset(fold[:], 0.0)
         quad = consts.tile([P, ROW_TILES], F32)
         nc.vector.tensor_reduce(
             out=quad[:], in_=ident[:].rearrange("p (t l) -> p t l", l=QUADRANT), axis=AXIS_X, op=ALU.add
@@ -99,8 +109,6 @@ def tile_wb_pa_t_kernel(tc, x, Wc_words, Wc_scales, bc, W1_words, W1_scales, b1,
         )
         quad_mean = consts.tile([P, ROW_TILES], F32)
         nc.vector.tensor_scalar_mul(out=quad_mean[:], in0=quad[:], scalar1=1.0 / PIXELS)
-        fold = consts.tile([P, PACK, QUADRANT, PACK], F32)
-        nc.vector.memset(fold[:], 0.0)
         for j in range(PACK):
             nc.vector.tensor_copy(out=fold[:, j, :, j], in_=lane[:])
 
@@ -110,8 +118,8 @@ def tile_wb_pa_t_kernel(tc, x, Wc_words, Wc_scales, bc, W1_words, W1_scales, b1,
         def over_pack(mask):
             return mask[:].unsqueeze(1).to_broadcast([P, PACK, ROW_TILES])
 
-        def move_to_rows(spread, name):
-            moved = moves.tile([P, ROW_TILES, RESULTS], F32, name=name)
+        def move_to_rows(spread):
+            moved = moves.tile([P, ROW_TILES, RESULTS], F32, name="moved")
             for j in range(PACK):
                 nc.tensor.matmul(
                     out=moved[:].rearrange("p t r -> p (t r)"),
@@ -127,127 +135,226 @@ def tile_wb_pa_t_kernel(tc, x, Wc_words, Wc_scales, bc, W1_words, W1_scales, b1,
             nc.gpsimd.tensor_tensor(
                 out=bias_spread[:, :, :, r], in0=over_tiles(bias4[r]), in1=over_pack(quad), op=ALU.mult
             )
-        bias_rows = move_to_rows(bias_spread, "bias_rows")
+        bias_moved = move_to_rows(bias_spread)
+        bias_rows = consts.tile([P, ROW_TILES, RESULTS], F32)
+        ident_bf = consts.tile([P, P], BF16)
+        make_identity(nc, ident_bf[:])
 
-        def prepare(b):
+        def sum_steps(b):
+            part = moves.tile([P, PACK, CHUNK], F32, name="part")
+            n_chunks = PIXELS // CHUNK
+
+            def step(i):
+                nc.tensor.matmul(
+                    out=part[:],
+                    lhsT=ident_bf[:],
+                    rhs=raws[b][:, :, i * CHUNK : (i + 1) * CHUNK],
+                    start=(i == 0),
+                    stop=(i == n_chunks - 1),
+                )
+
+            return part, [(step, i) for i in range(n_chunks)]
+
+        junk = consts.tile([P, PACK, PIXELS], BF16)
+
+        def steps_of(b):
             raw = raws[b]
-            sum4 = small.tile([P, PACK], F32, name="sum4")
-            max4 = small.tile([P, PACK], F32, name="max4")
-            top = work.tile([P, PACK, PIXELS // 2], BF16, name="top")
-            if b == 0:
-                waste = consts.tile([P, PACK, PIXELS], BF16, name="waste_scalar")
-            else:
-                waste = work.tile([P, PACK, PIXELS // 2], F32, name="waste_vector")
-            width = PIXELS // 2
-            for pair in ROW_PAIRS:
-                nc.vector.tensor_max(out=top[:, pair, :], in0=raw[:, pair, :width], in1=raw[:, pair, width:])
-            for j in range(PACK):
-                if b == 0:
-                    nc.scalar.activation(
-                        out=waste[:, j, :], in_=raw[:, j, :], func=IDENTITY, accum_out=sum4[:, j : j + 1]
-                    )
-                else:
-                    nc.vector.scalar_tensor_tensor(
-                        out=waste[:, j, :],
-                        in0=raw[:, j, : PIXELS // 2],
-                        scalar=1.0,
-                        in1=raw[:, j, PIXELS // 2 :],
-                        op0=ALU.mult,
-                        op1=ALU.add,
-                        accum_out=sum4[:, j : j + 1],
-                    )
-                if width > TREE_END:
-                    width //= 2
-                    nc.vector.tensor_max(
-                        out=top[:, :, :width], in0=top[:, :, :width], in1=top[:, :, width : 2 * width]
-                    )
-            assert width == TREE_END
-            nc.vector.tensor_reduce(out=max4[:], in_=top[:, :, :width], axis=AXIS_X, op=ALU.max)
+            img = {}
 
-            grouped = work.tile([P, PIXELS, PACK], BF16, align_bytes=64, name="grouped")
-            codes = work.tile([P, PIXELS], U32, align_bytes=64, name="codes")
-            scales = work.tile([P, PIXELS], U8, align_bytes=64, name="scales")
-            spread = small.tile([P, PACK, ROW_TILES, RESULTS], F32, name="spread")
+            def row_max(j):
+                nc.vector.tensor_scalar(
+                    out=junk[:, j, :],
+                    in0=raw[:, j, :],
+                    scalar1=1.0,
+                    scalar2=None,
+                    op0=ALU.mult,
+                    op1=ALU.max,
+                    accum_out=img["max4"][:, j : j + 1],
+                )
+
+            def begin():
+                img["sum4"] = small.tile([P, PACK], F32, name="sum4")
+                img["max4"] = small.tile([P, PACK], F32, name="max4")
+                img["grouped"] = work.tile([P, PIXELS, PACK], BF16, align_bytes=64, name="grouped")
+                img["codes"] = work.tile([P, PIXELS], U32, align_bytes=64, name="codes")
+                img["scales"] = work.tile([P, PIXELS], U8, align_bytes=64, name="scales")
+                img["spread"] = small.tile([P, PACK, ROW_TILES, RESULTS], F32, name="spread")
+
+            def sums_on_scalar():
+                waste = consts.tile([P, PACK, PIXELS], BF16, name="waste")
+                for j in range(PACK):
+                    nc.scalar.activation(
+                        out=waste[:, j, :], in_=raw[:, j, :], func=IDENTITY, accum_out=img["sum4"][:, j : j + 1]
+                    )
+
+            def take_sums(part):
+                nc.vector.tensor_reduce(out=img["sum4"][:], in_=part[:], axis=AXIS_X, op=ALU.add)
 
             def regroup(h):
                 cols = slice(h * N_PASS, (h + 1) * N_PASS)
                 nc.vector.tensor_copy(
-                    out=grouped[:, cols, :].rearrange("p (c i) j -> p c j i", i=RUN),
+                    out=img["grouped"][:, cols, :].rearrange("p (c i) j -> p c j i", i=RUN),
                     in_=raw[:, :, cols].rearrange("p j (c i) -> p c j i", i=RUN),
                 )
 
-            regroup(0)
-            nc.vector.scalar_tensor_tensor(
-                out=spread[:, :, :, 0],
-                in0=over_tiles(sum4),
-                scalar=PIXELS * EPS,
-                in1=over_pack(quad_mean),
-                op0=ALU.add,
-                op1=ALU.mult,
-            )
-            nc.vector.scalar_tensor_tensor(
-                out=spread[:, :, :, 1],
-                in0=over_tiles(max4),
-                scalar=EPS,
-                in1=over_pack(quad),
-                op0=ALU.add,
-                op1=ALU.mult,
-            )
-            divisors = move_to_rows(spread, "divisors")
-            regroup(1)
-            for h in range(HALVES):
+            def quantize(h):
                 cols = slice(h * N_PASS, (h + 1) * N_PASS)
                 nc.vector.quantize_mx(
-                    out=codes[:, cols].bitcast(FP8X4),
-                    scales=scales[:, cols],
-                    in_=grouped[:, cols, :].rearrange("p w j -> p (w j)"),
+                    out=img["codes"][:, cols].bitcast(FP8X4),
+                    scales=img["scales"][:, cols],
+                    in_=img["grouped"][:, cols, :].rearrange("p w j -> p (w j)"),
                 )
-            gain = small.tile([P, ROW_TILES, RESULTS], F32, name="gain")
-            nc.vector.reciprocal(out=gain[:], in_=divisors[:])
-            shift = small.tile([P, ROW_TILES, RESULTS], F32, name="shift")
-            nc.vector.tensor_mul(out=shift[:], in0=bias_rows[:], in1=gain[:])
-            return codes, scales, gain, shift
 
-        def multiply(b, prepared):
-            codes, scales, gain, shift = prepared
-            for r in range(RESULTS):
-                for t in range(ROW_TILES):
-                    rows = slice(t * P, (t + 1) * P)
-                    on_vector = b == IMAGES - 1 and t % 2 == 1
-                    done = results.tile([P, PIXELS], F32, name="done")
-                    for h in range(HALVES):
-                        cols = slice(h * N_PASS, (h + 1) * N_PASS)
-                        acc = banks.tile([P, N_PASS], F32, name="acc")
-                        nc.tensor.matmul_mx(
-                            out=acc[:],
-                            lhsT=w_words[:, r, rows].bitcast(FP8X4),
-                            lhsT_scale=w_scales[:, r, rows],
-                            rhs=codes[:, cols].bitcast(FP8X4),
-                            rhs_scale=scales[:, cols],
-                            start=True,
-                            stop=True,
-                        )
-                        if on_vector:
-                            nc.vector.tensor_scalar(
-                                out=done[:, cols],
-                                in0=acc[:],
-                                scalar1=gain[:, t, r : r + 1],
-                                scalar2=shift[:, t, r : r + 1],
-                                op0=ALU.mult,
-                                op1=ALU.add,
-                            )
-                        else:
-                            nc.scalar.activation(
-                                out=done[:, cols],
-                                in_=acc[:],
-                                func=IDENTITY,
-                                bias=shift[:, t, r : r + 1],
-                                scale=gain[:, t, r : r + 1],
-                            )
-                    nc.sync.dma_start(out=outs[r][b, rows].rearrange("c h w -> c (h w)"), in_=done[:])
+            def spread_max():
+                nc.vector.scalar_tensor_tensor(
+                    out=img["spread"][:, :, :, 1],
+                    in0=over_tiles(img["max4"]),
+                    scalar=EPS,
+                    in1=over_pack(quad),
+                    op0=ALU.add,
+                    op1=ALU.mult,
+                )
 
-        prepared = prepare(0)
+            def spread_sum():
+                nc.vector.scalar_tensor_tensor(
+                    out=img["spread"][:, :, :, 0],
+                    in0=over_tiles(img["sum4"]),
+                    scalar=PIXELS * EPS,
+                    in1=over_pack(quad_mean),
+                    op0=ALU.add,
+                    op1=ALU.mult,
+                )
+                return move_to_rows(img["spread"])
+
+            def finish(divisors):
+                img["gain"] = small.tile([P, ROW_TILES, RESULTS], F32, name="gain")
+                img["shift"] = small.tile([P, ROW_TILES, RESULTS], F32, name="shift")
+                nc.vector.reciprocal(out=img["gain"][:], in_=divisors[:])
+                nc.vector.tensor_mul(out=img["shift"][:], in0=bias_rows[:], in1=img["gain"][:])
+
+            img["row_max"] = row_max
+            img["begin"] = begin
+            img["sums_on_scalar"] = sums_on_scalar
+            img["take_sums"] = take_sums
+            img["regroup"] = regroup
+            img["quantize"] = quantize
+            img["spread_max"] = spread_max
+            img["spread_sum"] = spread_sum
+            img["finish"] = finish
+            return img
+
+        def one_pass(img, r, t, h):
+            acc = banks.tile([P, N_PASS], F32, name="acc")
+            cols = slice(h * N_PASS, (h + 1) * N_PASS)
+            rows = slice(t * P, (t + 1) * P)
+            nc.tensor.matmul_mx(
+                out=acc[:],
+                lhsT=w_words[:, r, rows].bitcast(FP8X4),
+                lhsT_scale=w_scales[:, r, rows],
+                rhs=img["codes"][:, cols].bitcast(FP8X4),
+                rhs_scale=img["scales"][:, cols],
+                start=True,
+                stop=True,
+            )
+            return acc
+
+        def empty(on_vector, img, acc, done, r, t, h):
+            cols = slice(h * N_PASS, (h + 1) * N_PASS)
+            if on_vector:
+                nc.vector.tensor_scalar(
+                    out=done[:, cols],
+                    in0=acc[:],
+                    scalar1=img["gain"][:, t, r : r + 1],
+                    scalar2=img["shift"][:, t, r : r + 1],
+                    op0=ALU.mult,
+                    op1=ALU.add,
+                )
+            else:
+                nc.scalar.activation(
+                    out=done[:, cols],
+                    in_=acc[:],
+                    func=IDENTITY,
+                    bias=img["shift"][:, t, r : r + 1],
+                    scale=img["gain"][:, t, r : r + 1],
+                )
+
+        def store(b, r, t, done, h):
+            rows_out = outs[r][b, t * P : (t + 1) * P].rearrange("c h w -> c (h w)")
+            if h is None:
+                nc.sync.dma_start(out=rows_out, in_=done[:])
+            else:
+                cols = slice(h * N_PASS, (h + 1) * N_PASS)
+                nc.sync.dma_start(out=rows_out[:, cols], in_=done[:, cols])
+
+        imgs = [steps_of(b) for b in range(IMAGES)]
+        img = imgs[0]
+        img["begin"]()
+        img["sums_on_scalar"]()
+        for j in range(PACK):
+            img["row_max"](j)
+        img["regroup"](0)
+        img["spread_max"]()
+        nc.vector.tensor_copy(out=bias_rows[:], in_=bias_moved[:])
+        img["quantize"](0)
+        divisors = img["spread_sum"]()
+        img["regroup"](1)
+        img["finish"](divisors)
+        img["quantize"](1)
+
+        plain_order = [(r, t, h) for r in range(RESULTS) for t in range(ROW_TILES) for h in range(HALVES)]
         for b in range(IMAGES):
-            multiply(b, prepared)
-            if b + 1 < IMAGES:
-                prepared = prepare(b + 1)
+            img = imgs[b]
+            last = b == IMAGES - 1
+            halves_leave = 4 if b == 0 else 0
+            order = [(0, 0, 0), (0, 1, 0), (0, 0, 1), (0, 1, 1)] + plain_order[4:] if b == 0 else plain_order
+            dones = {}
+            filled = {}
+
+            def run(k):
+                r, t, h = order[k]
+                if (r, t) not in dones:
+                    dones[(r, t)] = results.tile([P, PIXELS], F32, name="done")
+                    filled[(r, t)] = 0
+                return one_pass(img, r, t, h)
+
+            def leave(k, on_vector, acc):
+                r, t, h = order[k]
+                empty(on_vector, img, acc, dones[(r, t)], r, t, h)
+                filled[(r, t)] += 1
+                if k < halves_leave:
+                    store(b, r, t, dones[(r, t)], h)
+                elif filled[(r, t)] == HALVES:
+                    store(b, r, t, dones[(r, t)], None)
+
+            if last:
+                for k in range(PASSES):
+                    leave(k, k % 2 == 1, run(k))
+                continue
+
+            nxt = imgs[b + 1]
+            part, woven = sum_steps(b + 1)
+            for k in range(EARLY_BANK):
+                acc = run(k)
+                if k + 1 >= LEAD and woven:
+                    step, i = woven.pop(0)
+                    step(i)
+                leave(k, False, acc)
+            assert not woven
+            accs = []
+            nxt["begin"]()
+            nxt["regroup"](0)
+            for j in range(PACK):
+                nxt["row_max"](j)
+            nxt["quantize"](0)
+            for k in range(EARLY_BANK, PASSES):
+                accs.append(run(k))
+                if k not in (EARLY_BANK, PASSES - 1):
+                    leave(k, False, accs[k - EARLY_BANK])
+            nxt["take_sums"](part)
+            nxt["spread_max"]()
+            divisors = nxt["spread_sum"]()
+            nxt["regroup"](1)
+            leave(EARLY_BANK, True, accs[0])
+            nxt["quantize"](1)
+            nxt["finish"](divisors)
+            leave(PASSES - 1, True, accs[PASSES - 1 - EARLY_BANK])

@@ -29,6 +29,8 @@ ROW_PAIRS = (slice(0, 2), slice(2, 4))
 ROWS_ALONE = (slice(0, 1), slice(1, 2), slice(2, 3), slice(3, 4))
 CHUNK = 128
 LEAD = 3
+BOTH = slice(0, 2)
+WITH_BIASES = slice(0, 4)
 PASSES = RESULTS * ROW_TILES * HALVES
 EARLY_BANK = 12
 
@@ -97,8 +99,6 @@ def tile_wb_pa_t_kernel(tc, x, Wc_words, Wc_scales, bc, W1_words, W1_scales, b1,
 
         ident = consts.tile([P, P], F32)
         make_identity(nc, ident[:])
-        fold = consts.tile([P, PACK, QUADRANT, PACK], F32)
-        nc.vector.memset(fold[:], 0.0)
         quad = consts.tile([P, ROW_TILES], F32)
         nc.vector.tensor_reduce(
             out=quad[:], in_=ident[:].rearrange("p (t l) -> p t l", l=QUADRANT), axis=AXIS_X, op=ALU.add
@@ -107,10 +107,14 @@ def tile_wb_pa_t_kernel(tc, x, Wc_words, Wc_scales, bc, W1_words, W1_scales, b1,
         nc.vector.tensor_reduce(
             out=lane[:], in_=ident[:].rearrange("p (t l) -> p l t", l=QUADRANT), axis=AXIS_X, op=ALU.add
         )
+        pick = consts.tile([P, PACK], F32)
+        nc.vector.tensor_reduce(
+            out=pick[:], in_=ident[:].rearrange("p (l j) -> p j l", j=PACK), axis=AXIS_X, op=ALU.add
+        )
+        fold = consts.tile([P, QUADRANT, PACK], F32)
+        nc.vector.tensor_copy(out=fold[:], in_=lane[:].unsqueeze(2).to_broadcast([P, QUADRANT, PACK]))
         quad_mean = consts.tile([P, ROW_TILES], F32)
         nc.vector.tensor_scalar_mul(out=quad_mean[:], in0=quad[:], scalar1=1.0 / PIXELS)
-        for j in range(PACK):
-            nc.vector.tensor_copy(out=fold[:, j, :, j], in_=lane[:])
 
         def over_tiles(vec4):
             return vec4[:].unsqueeze(2).to_broadcast([P, PACK, ROW_TILES])
@@ -118,25 +122,39 @@ def tile_wb_pa_t_kernel(tc, x, Wc_words, Wc_scales, bc, W1_words, W1_scales, b1,
         def over_pack(mask):
             return mask[:].unsqueeze(1).to_broadcast([P, PACK, ROW_TILES])
 
-        def move_to_rows(spread):
-            moved = moves.tile([P, ROW_TILES, RESULTS], F32, name="moved")
-            for j in range(PACK):
-                nc.tensor.matmul(
-                    out=moved[:].rearrange("p t r -> p (t r)"),
-                    lhsT=fold[:, j, :, :].rearrange("p l i -> p (l i)"),
-                    rhs=spread[:, j, :, :].rearrange("p t r -> p (t r)"),
-                    start=(j == 0),
-                    stop=(j == PACK - 1),
-                )
-            return moved
+        def n_of(some):
+            return some.stop - some.start
 
-        bias_spread = consts.tile([P, PACK, ROW_TILES, RESULTS], F32)
+        def move_to_rows(spread, moved, some):
+            nc.tensor.matmul(
+                out=moved[:, some, :, :].rearrange("p r j t -> p (r j t)"),
+                lhsT=fold[:].rearrange("p l i -> p (l i)"),
+                rhs=spread[:, some, :, :].rearrange("p r j t -> p (r j t)"),
+                start=True,
+                stop=True,
+            )
+
+        def mask_rows(masked, moved, some):
+            nc.vector.tensor_tensor(
+                out=masked[:, some, :, :],
+                in0=moved[:, some, :, :],
+                in1=pick[:].unsqueeze(1).unsqueeze(3).to_broadcast([P, n_of(some), PACK, ROW_TILES]),
+                op=ALU.mult,
+            )
+
+        def take_rows(rows, masked, some):
+            nc.vector.tensor_reduce(
+                out=rows[:, some, :], in_=masked[:, some, :, :].rearrange("p r j t -> p r t j"), axis=AXIS_X, op=ALU.add
+            )
+
+        first_spread = consts.tile([P, 2 * RESULTS, PACK, ROW_TILES], F32)
+        first_masked = consts.tile([P, 2 * RESULTS, PACK, ROW_TILES], F32)
+        first_rows = consts.tile([P, 2 * RESULTS, ROW_TILES], F32)
         for r in range(RESULTS):
             nc.gpsimd.tensor_tensor(
-                out=bias_spread[:, :, :, r], in0=over_tiles(bias4[r]), in1=over_pack(quad), op=ALU.mult
+                out=first_spread[:, RESULTS + r, :, :], in0=over_tiles(bias4[r]), in1=over_pack(quad), op=ALU.mult
             )
-        bias_moved = move_to_rows(bias_spread)
-        bias_rows = consts.tile([P, ROW_TILES, RESULTS], F32)
+        bias_rows = first_rows[:, RESULTS:, :]
         ident_bf = consts.tile([P, P], BF16)
         make_identity(nc, ident_bf[:])
 
@@ -155,6 +173,7 @@ def tile_wb_pa_t_kernel(tc, x, Wc_words, Wc_scales, bc, W1_words, W1_scales, b1,
 
             return part, [(step, i) for i in range(n_chunks)]
 
+        halves = consts.tile([P, PIXELS // 2], F32)
         junk = consts.tile([P, PACK, PIXELS], BF16)
 
         def steps_of(b):
@@ -178,14 +197,33 @@ def tile_wb_pa_t_kernel(tc, x, Wc_words, Wc_scales, bc, W1_words, W1_scales, b1,
                 img["grouped"] = work.tile([P, PIXELS, PACK], BF16, align_bytes=64, name="grouped")
                 img["codes"] = work.tile([P, PIXELS], U32, align_bytes=64, name="codes")
                 img["scales"] = work.tile([P, PIXELS], U8, align_bytes=64, name="scales")
-                img["spread"] = small.tile([P, PACK, ROW_TILES, RESULTS], F32, name="spread")
+                if b == 0:
+                    img["spread"], img["masked"], img["den"] = first_spread, first_masked, first_rows
+                else:
+                    img["spread"] = small.tile([P, RESULTS, PACK, ROW_TILES], F32, name="spread")
+                    img["masked"] = small.tile([P, RESULTS, PACK, ROW_TILES], F32, name="masked")
+                    img["den"] = small.tile([P, RESULTS, ROW_TILES], F32, name="den")
+                img["gain"] = small.tile([P, RESULTS, ROW_TILES], F32, name="gain")
+                img["shift"] = small.tile([P, RESULTS, ROW_TILES], F32, name="shift")
 
             def sums_on_scalar():
                 waste = consts.tile([P, PACK, PIXELS], BF16, name="waste")
-                for j in range(PACK):
+                for j in range(PACK - 1):
                     nc.scalar.activation(
                         out=waste[:, j, :], in_=raw[:, j, :], func=IDENTITY, accum_out=img["sum4"][:, j : j + 1]
                     )
+
+            def last_sum_on_vector():
+                j = PACK - 1
+                nc.vector.scalar_tensor_tensor(
+                    out=halves[:],
+                    in0=raw[:, j, : PIXELS // 2],
+                    scalar=1.0,
+                    in1=raw[:, j, PIXELS // 2 :],
+                    op0=ALU.mult,
+                    op1=ALU.add,
+                    accum_out=img["sum4"][:, j : j + 1],
+                )
 
             def take_sums(part):
                 nc.vector.tensor_reduce(out=img["sum4"][:], in_=part[:], axis=AXIS_X, op=ALU.add)
@@ -207,7 +245,7 @@ def tile_wb_pa_t_kernel(tc, x, Wc_words, Wc_scales, bc, W1_words, W1_scales, b1,
 
             def spread_max():
                 nc.vector.scalar_tensor_tensor(
-                    out=img["spread"][:, :, :, 1],
+                    out=img["spread"][:, 1, :, :],
                     in0=over_tiles(img["max4"]),
                     scalar=EPS,
                     in1=over_pack(quad),
@@ -217,30 +255,46 @@ def tile_wb_pa_t_kernel(tc, x, Wc_words, Wc_scales, bc, W1_words, W1_scales, b1,
 
             def spread_sum():
                 nc.vector.scalar_tensor_tensor(
-                    out=img["spread"][:, :, :, 0],
+                    out=img["spread"][:, 0, :, :],
                     in0=over_tiles(img["sum4"]),
                     scalar=PIXELS * EPS,
                     in1=over_pack(quad_mean),
                     op0=ALU.add,
                     op1=ALU.mult,
                 )
-                return move_to_rows(img["spread"])
 
-            def finish(divisors):
-                img["gain"] = small.tile([P, ROW_TILES, RESULTS], F32, name="gain")
-                img["shift"] = small.tile([P, ROW_TILES, RESULTS], F32, name="shift")
-                nc.vector.reciprocal(out=img["gain"][:], in_=divisors[:])
-                nc.vector.tensor_mul(out=img["shift"][:], in0=bias_rows[:], in1=img["gain"][:])
+            def move(some):
+                img["moved"] = moves.tile([P, n_of(some), PACK, ROW_TILES], F32, name="moved")
+                move_to_rows(img["spread"], img["moved"], some)
+
+            def mask(some):
+                mask_rows(img["masked"], img["moved"], some)
+
+            def take(some):
+                take_rows(img["den"], img["masked"], some)
+
+            def invert(some):
+                nc.vector.reciprocal(out=img["gain"][:, some, :], in_=img["den"][:, some, :])
+
+            def scale_bias(some):
+                nc.vector.tensor_mul(
+                    out=img["shift"][:, some, :], in0=bias_rows, in1=img["gain"][:, some, :]
+                )
 
             img["row_max"] = row_max
             img["begin"] = begin
             img["sums_on_scalar"] = sums_on_scalar
+            img["last_sum_on_vector"] = last_sum_on_vector
             img["take_sums"] = take_sums
             img["regroup"] = regroup
             img["quantize"] = quantize
             img["spread_max"] = spread_max
             img["spread_sum"] = spread_sum
-            img["finish"] = finish
+            img["move"] = move
+            img["mask"] = mask
+            img["take"] = take
+            img["invert"] = invert
+            img["scale_bias"] = scale_bias
             return img
 
         def one_pass(img, r, t, h):
@@ -264,8 +318,8 @@ def tile_wb_pa_t_kernel(tc, x, Wc_words, Wc_scales, bc, W1_words, W1_scales, b1,
                 nc.vector.tensor_scalar(
                     out=done[:, cols],
                     in0=acc[:],
-                    scalar1=img["gain"][:, t, r : r + 1],
-                    scalar2=img["shift"][:, t, r : r + 1],
+                    scalar1=img["gain"][:, r, t : t + 1],
+                    scalar2=img["shift"][:, r, t : t + 1],
                     op0=ALU.mult,
                     op1=ALU.add,
                 )
@@ -274,8 +328,8 @@ def tile_wb_pa_t_kernel(tc, x, Wc_words, Wc_scales, bc, W1_words, W1_scales, b1,
                     out=done[:, cols],
                     in_=acc[:],
                     func=IDENTITY,
-                    bias=img["shift"][:, t, r : r + 1],
-                    scale=img["gain"][:, t, r : r + 1],
+                    bias=img["shift"][:, r, t : t + 1],
+                    scale=img["gain"][:, r, t : t + 1],
                 )
 
         def store(b, r, t, done, h):
@@ -292,21 +346,27 @@ def tile_wb_pa_t_kernel(tc, x, Wc_words, Wc_scales, bc, W1_words, W1_scales, b1,
         img["sums_on_scalar"]()
         for j in range(PACK):
             img["row_max"](j)
-        img["regroup"](0)
+        img["last_sum_on_vector"]()
         img["spread_max"]()
-        nc.vector.tensor_copy(out=bias_rows[:], in_=bias_moved[:])
+        img["spread_sum"]()
+        img["move"](WITH_BIASES)
+        img["regroup"](0)
+        img["mask"](WITH_BIASES)
         img["quantize"](0)
-        divisors = img["spread_sum"]()
+        img["take"](WITH_BIASES)
+        img["invert"](BOTH)
+        img["scale_bias"](BOTH)
         img["regroup"](1)
-        img["finish"](divisors)
         img["quantize"](1)
 
         plain_order = [(r, t, h) for r in range(RESULTS) for t in range(ROW_TILES) for h in range(HALVES)]
         for b in range(IMAGES):
             img = imgs[b]
             last = b == IMAGES - 1
-            halves_leave = 4 if b == 0 else 0
-            order = [(0, 0, 0), (0, 1, 0), (0, 0, 1), (0, 1, 1)] + plain_order[4:] if b == 0 else plain_order
+            halves_leave = PASSES // 2 if b == 0 else 0
+            order = plain_order
+            if b == 0:
+                order = [(0, t, h) for h in range(HALVES) for t in range(ROW_TILES)] + plain_order[PASSES // 2 :]
             dones = {}
             filled = {}
 
@@ -333,28 +393,35 @@ def tile_wb_pa_t_kernel(tc, x, Wc_words, Wc_scales, bc, W1_words, W1_scales, b1,
 
             nxt = imgs[b + 1]
             part, woven = sum_steps(b + 1)
-            for k in range(EARLY_BANK):
+            for k in range(PASSES // 2):
                 acc = run(k)
-                if k + 1 >= LEAD and woven:
+                if k + 1 >= LEAD:
                     step, i = woven.pop(0)
                     step(i)
                 leave(k, False, acc)
-            assert not woven
-            accs = []
             nxt["begin"]()
             nxt["regroup"](0)
             for j in range(PACK):
                 nxt["row_max"](j)
             nxt["quantize"](0)
-            for k in range(EARLY_BANK, PASSES):
-                accs.append(run(k))
+            accs = {}
+            for k in range(PASSES // 2, PASSES):
+                accs[k] = run(k)
+                if woven:
+                    step, i = woven.pop(0)
+                    step(i)
                 if k not in (EARLY_BANK, PASSES - 1):
-                    leave(k, False, accs[k - EARLY_BANK])
+                    leave(k, False, accs[k])
+            assert not woven
             nxt["take_sums"](part)
             nxt["spread_max"]()
-            divisors = nxt["spread_sum"]()
+            nxt["spread_sum"]()
+            nxt["move"](BOTH)
             nxt["regroup"](1)
-            leave(EARLY_BANK, True, accs[0])
+            nxt["mask"](BOTH)
             nxt["quantize"](1)
-            nxt["finish"](divisors)
-            leave(PASSES - 1, True, accs[PASSES - 1 - EARLY_BANK])
+            nxt["take"](BOTH)
+            leave(EARLY_BANK, True, accs[EARLY_BANK])
+            nxt["invert"](BOTH)
+            leave(PASSES - 1, True, accs[PASSES - 1])
+            nxt["scale_bias"](BOTH)

@@ -27,6 +27,7 @@ EPS = 1e-5
 RUN = 4
 ROW_PAIRS = (slice(0, 2), slice(2, 4))
 ROWS_ALONE = (slice(0, 1), slice(1, 2), slice(2, 3), slice(3, 4))
+ALL_ROWS = slice(0, 4)
 CHUNK = 128
 LEAD = 3
 BOTH = slice(0, 2)
@@ -71,7 +72,7 @@ def tile_wb_pa_t_kernel(tc, x, Wc_words, Wc_scales, bc, W1_words, W1_scales, b1,
         def load_image(b):
             raw = images.tile([P, PACK, PIXELS], BF16, name="raw")
             rows_of_p = x[b].rearrange("(p j) h w -> p j (h w)", j=PACK)
-            for part_of in ROWS_ALONE if b == 0 else ROW_PAIRS:
+            for part_of in ROWS_ALONE if b == 0 else (ALL_ROWS,):
                 nc.sync.dma_start(out=raw[:, part_of, :], in_=rows_of_p[:, part_of, :])
             return raw
 
@@ -89,12 +90,12 @@ def tile_wb_pa_t_kernel(tc, x, Wc_words, Wc_scales, bc, W1_words, W1_scales, b1,
             )
 
         raws = [load_image(0)]
-        load_scales(0)
         load_words(0)
         raws.append(load_image(1))
+        load_scales(0)
         load_words(1)
-        load_scales(1)
         raws.append(load_image(2))
+        load_scales(1)
         raws.append(load_image(3))
 
         ident = consts.tile([P, P], F32)
@@ -410,7 +411,7 @@ def tile_wb_pa_t_kernel(tc, x, Wc_words, Wc_scales, bc, W1_words, W1_scales, b1,
                 if woven:
                     step, i = woven.pop(0)
                     step(i)
-                if k not in (EARLY_BANK, PASSES - 1):
+                if k != PASSES - 1:
                     leave(k, False, accs[k])
             assert not woven
             nxt["take_sums"](part)
@@ -421,7 +422,6 @@ def tile_wb_pa_t_kernel(tc, x, Wc_words, Wc_scales, bc, W1_words, W1_scales, b1,
             nxt["mask"](BOTH)
             nxt["quantize"](1)
             nxt["take"](BOTH)
-            leave(EARLY_BANK, True, accs[EARLY_BANK])
-            nxt["invert"](BOTH)
             leave(PASSES - 1, True, accs[PASSES - 1])
+            nxt["invert"](BOTH)
             nxt["scale_bias"](BOTH)

@@ -28,12 +28,13 @@ RUN = 4
 ROW_PAIRS = (slice(0, 2), slice(2, 4))
 ROWS_ALONE = (slice(0, 1), slice(1, 2), slice(2, 3), slice(3, 4))
 ALL_ROWS = slice(0, 4)
-CHUNK = 128
+CHUNK = 64
+WEAVE = 2
 LEAD = 3
 BOTH = slice(0, 2)
 WITH_BIASES = slice(0, 4)
 PASSES = RESULTS * ROW_TILES * HALVES
-EARLY_BANK = 12
+MOVE_BEHIND = 12
 
 FLOPS = 2 * RESULTS * IMAGES * CHANNELS * CHANNELS * PIXELS
 
@@ -158,6 +159,10 @@ def tile_wb_pa_t_kernel(tc, x, Wc_words, Wc_scales, bc, W1_words, W1_scales, b1,
         bias_rows = first_rows[:, RESULTS:, :]
         ident_bf = consts.tile([P, P], BF16)
         make_identity(nc, ident_bf[:])
+        averager = consts.tile([P, P], BF16)
+        nc.gpsimd.tensor_scalar(
+            out=averager[:], in0=ident_bf[:], scalar1=1.0 / PIXELS, scalar2=0.0, op0=ALU.mult, op1=ALU.add
+        )
 
         def sum_steps(b):
             part = moves.tile([P, PACK, CHUNK], F32, name="part")
@@ -166,7 +171,7 @@ def tile_wb_pa_t_kernel(tc, x, Wc_words, Wc_scales, bc, W1_words, W1_scales, b1,
             def step(i):
                 nc.tensor.matmul(
                     out=part[:],
-                    lhsT=ident_bf[:],
+                    lhsT=averager[:],
                     rhs=raws[b][:, :, i * CHUNK : (i + 1) * CHUNK],
                     start=(i == 0),
                     stop=(i == n_chunks - 1),
@@ -189,12 +194,11 @@ def tile_wb_pa_t_kernel(tc, x, Wc_words, Wc_scales, bc, W1_words, W1_scales, b1,
                     scalar2=None,
                     op0=ALU.mult,
                     op1=ALU.max,
-                    accum_out=img["max4"][:, j : j + 1],
+                    accum_out=img["stat"][:, 1, j : j + 1],
                 )
 
             def begin():
-                img["sum4"] = small.tile([P, PACK], F32, name="sum4")
-                img["max4"] = small.tile([P, PACK], F32, name="max4")
+                img["stat"] = small.tile([P, RESULTS, PACK], F32, name="stat")
                 img["grouped"] = work.tile([P, PIXELS, PACK], BF16, align_bytes=64, name="grouped")
                 img["codes"] = work.tile([P, PIXELS], U32, align_bytes=64, name="codes")
                 img["scales"] = work.tile([P, PIXELS], U8, align_bytes=64, name="scales")
@@ -211,7 +215,7 @@ def tile_wb_pa_t_kernel(tc, x, Wc_words, Wc_scales, bc, W1_words, W1_scales, b1,
                 waste = consts.tile([P, PACK, PIXELS], BF16, name="waste")
                 for j in range(PACK - 1):
                     nc.scalar.activation(
-                        out=waste[:, j, :], in_=raw[:, j, :], func=IDENTITY, accum_out=img["sum4"][:, j : j + 1]
+                        out=waste[:, j, :], in_=raw[:, j, :], func=IDENTITY, accum_out=img["stat"][:, 0, j : j + 1]
                     )
 
             def last_sum_on_vector():
@@ -223,15 +227,33 @@ def tile_wb_pa_t_kernel(tc, x, Wc_words, Wc_scales, bc, W1_words, W1_scales, b1,
                     in1=raw[:, j, PIXELS // 2 :],
                     op0=ALU.mult,
                     op1=ALU.add,
-                    accum_out=img["sum4"][:, j : j + 1],
+                    accum_out=img["stat"][:, 0, j : j + 1],
                 )
 
-            def take_sums(part):
-                nc.vector.tensor_reduce(out=img["sum4"][:], in_=part[:], axis=AXIS_X, op=ALU.add)
+            def take_means(part):
+                nc.vector.tensor_reduce(out=img["stat"][:, 0, :], in_=part[:], axis=AXIS_X, op=ALU.add)
+
+            def spread_both():
+                groups = RESULTS * PACK
+                nc.vector.scalar_tensor_tensor(
+                    out=img["spread"][:].rearrange("p r j t -> p (r j) t"),
+                    in0=img["stat"][:].rearrange("p r j -> p (r j)").unsqueeze(2).to_broadcast([P, groups, ROW_TILES]),
+                    scalar=EPS,
+                    in1=quad[:].unsqueeze(1).to_broadcast([P, groups, ROW_TILES]),
+                    op0=ALU.add,
+                    op1=ALU.mult,
+                )
 
             def regroup(h):
                 cols = slice(h * N_PASS, (h + 1) * N_PASS)
                 nc.vector.tensor_copy(
+                    out=img["grouped"][:, cols, :].rearrange("p (c i) j -> p c j i", i=RUN),
+                    in_=raw[:, :, cols].rearrange("p j (c i) -> p c j i", i=RUN),
+                )
+
+            def regroup_on_scalar(h):
+                cols = slice(h * N_PASS, (h + 1) * N_PASS)
+                nc.scalar.copy(
                     out=img["grouped"][:, cols, :].rearrange("p (c i) j -> p c j i", i=RUN),
                     in_=raw[:, :, cols].rearrange("p j (c i) -> p c j i", i=RUN),
                 )
@@ -247,7 +269,7 @@ def tile_wb_pa_t_kernel(tc, x, Wc_words, Wc_scales, bc, W1_words, W1_scales, b1,
             def spread_max():
                 nc.vector.scalar_tensor_tensor(
                     out=img["spread"][:, 1, :, :],
-                    in0=over_tiles(img["max4"]),
+                    in0=img["stat"][:, 1, :].unsqueeze(2).to_broadcast([P, PACK, ROW_TILES]),
                     scalar=EPS,
                     in1=over_pack(quad),
                     op0=ALU.add,
@@ -257,7 +279,7 @@ def tile_wb_pa_t_kernel(tc, x, Wc_words, Wc_scales, bc, W1_words, W1_scales, b1,
             def spread_sum():
                 nc.vector.scalar_tensor_tensor(
                     out=img["spread"][:, 0, :, :],
-                    in0=over_tiles(img["sum4"]),
+                    in0=img["stat"][:, 0, :].unsqueeze(2).to_broadcast([P, PACK, ROW_TILES]),
                     scalar=PIXELS * EPS,
                     in1=over_pack(quad_mean),
                     op0=ALU.add,
@@ -286,8 +308,10 @@ def tile_wb_pa_t_kernel(tc, x, Wc_words, Wc_scales, bc, W1_words, W1_scales, b1,
             img["begin"] = begin
             img["sums_on_scalar"] = sums_on_scalar
             img["last_sum_on_vector"] = last_sum_on_vector
-            img["take_sums"] = take_sums
+            img["take_means"] = take_means
+            img["spread_both"] = spread_both
             img["regroup"] = regroup
+            img["regroup_on_scalar"] = regroup_on_scalar
             img["quantize"] = quantize
             img["spread_max"] = spread_max
             img["spread_sum"] = spread_sum
@@ -345,6 +369,7 @@ def tile_wb_pa_t_kernel(tc, x, Wc_words, Wc_scales, bc, W1_words, W1_scales, b1,
         img = imgs[0]
         img["begin"]()
         img["sums_on_scalar"]()
+        img["regroup_on_scalar"](1)
         for j in range(PACK):
             img["row_max"](j)
         img["last_sum_on_vector"]()
@@ -357,7 +382,6 @@ def tile_wb_pa_t_kernel(tc, x, Wc_words, Wc_scales, bc, W1_words, W1_scales, b1,
         img["take"](WITH_BIASES)
         img["invert"](BOTH)
         img["scale_bias"](BOTH)
-        img["regroup"](1)
         img["quantize"](1)
 
         plain_order = [(r, t, h) for r in range(RESULTS) for t in range(ROW_TILES) for h in range(HALVES)]
@@ -397,31 +421,35 @@ def tile_wb_pa_t_kernel(tc, x, Wc_words, Wc_scales, bc, W1_words, W1_scales, b1,
             for k in range(PASSES // 2):
                 acc = run(k)
                 if k + 1 >= LEAD:
-                    step, i = woven.pop(0)
-                    step(i)
+                    for step, i in woven[:WEAVE]:
+                        step(i)
+                    woven = woven[WEAVE:]
                 leave(k, False, acc)
             nxt["begin"]()
             nxt["regroup"](0)
             for j in range(PACK):
                 nxt["row_max"](j)
-            nxt["quantize"](0)
+            mine = (PASSES - 1,) if b == 0 else (PASSES - 2, PASSES - 1)
             accs = {}
             for k in range(PASSES // 2, PASSES):
                 accs[k] = run(k)
-                if woven:
-                    step, i = woven.pop(0)
+                for step, i in woven[:WEAVE]:
                     step(i)
-                if k != PASSES - 1:
+                woven = woven[WEAVE:]
+                if k not in mine:
                     leave(k, False, accs[k])
-            assert not woven
-            nxt["take_sums"](part)
-            nxt["spread_max"]()
-            nxt["spread_sum"]()
-            nxt["move"](BOTH)
+                if k == MOVE_BEHIND:
+                    assert not woven
+                    nxt["take_means"](part)
+                    nxt["quantize"](0)
+                    nxt["spread_both"]()
+                    nxt["move"](BOTH)
             nxt["regroup"](1)
             nxt["mask"](BOTH)
             nxt["quantize"](1)
             nxt["take"](BOTH)
-            leave(PASSES - 1, True, accs[PASSES - 1])
+            if len(mine) == 2:
+                leave(mine[0], True, accs[mine[0]])
             nxt["invert"](BOTH)
+            leave(PASSES - 1, True, accs[PASSES - 1])
             nxt["scale_bias"](BOTH)

@@ -180,6 +180,7 @@ def tile_wb_pa_t_kernel(tc, x, Wc_words, Wc_scales, bc, W1_words, W1_scales, b1,
             return part, [(step, i) for i in range(n_chunks)]
 
         halves = consts.tile([P, PIXELS // 2], F32)
+        go = consts.tile([P, IMAGES], F32)
         junk = consts.tile([P, PACK, PIXELS], BF16)
 
         def steps_of(b):
@@ -258,6 +259,20 @@ def tile_wb_pa_t_kernel(tc, x, Wc_words, Wc_scales, bc, W1_words, W1_scales, b1,
                     in_=raw[:, :, cols].rearrange("p j (c i) -> p c j i", i=RUN),
                 )
 
+            def signal_gpsimd():
+                nc.vector.memset(go[:, b : b + 1], 1.0)
+
+            def regroup_on_gpsimd(h):
+                cols = slice(h * N_PASS, (h + 1) * N_PASS)
+                nc.gpsimd.tensor_scalar(
+                    out=img["grouped"][:, cols, :],
+                    in0=raw[:, :, cols].rearrange("p j w -> p w j"),
+                    scalar1=go[:, b : b + 1],
+                    scalar2=0.0,
+                    op0=ALU.mult,
+                    op1=ALU.add,
+                )
+
             def quantize(h):
                 cols = slice(h * N_PASS, (h + 1) * N_PASS)
                 nc.vector.quantize_mx(
@@ -313,6 +328,8 @@ def tile_wb_pa_t_kernel(tc, x, Wc_words, Wc_scales, bc, W1_words, W1_scales, b1,
             img["regroup"] = regroup
             img["regroup_on_scalar"] = regroup_on_scalar
             img["quantize"] = quantize
+            img["signal_gpsimd"] = signal_gpsimd
+            img["regroup_on_gpsimd"] = regroup_on_gpsimd
             img["spread_max"] = spread_max
             img["spread_sum"] = spread_sum
             img["move"] = move
@@ -427,6 +444,8 @@ def tile_wb_pa_t_kernel(tc, x, Wc_words, Wc_scales, bc, W1_words, W1_scales, b1,
                 leave(k, False, acc)
             nxt["begin"]()
             nxt["regroup"](0)
+            nxt["signal_gpsimd"]()
+            nxt["regroup_on_gpsimd"](1)
             for j in range(PACK):
                 nxt["row_max"](j)
             mine = (PASSES - 1,) if b == 0 else (PASSES - 2, PASSES - 1)
@@ -444,12 +463,11 @@ def tile_wb_pa_t_kernel(tc, x, Wc_words, Wc_scales, bc, W1_words, W1_scales, b1,
                     nxt["quantize"](0)
                     nxt["spread_both"]()
                     nxt["move"](BOTH)
-            nxt["regroup"](1)
-            nxt["mask"](BOTH)
             nxt["quantize"](1)
-            nxt["take"](BOTH)
+            nxt["mask"](BOTH)
             if len(mine) == 2:
                 leave(mine[0], True, accs[mine[0]])
-            nxt["invert"](BOTH)
+            nxt["take"](BOTH)
             leave(PASSES - 1, True, accs[PASSES - 1])
+            nxt["invert"](BOTH)
             nxt["scale_bias"](BOTH)

from contextlib import ExitStack

import concourse.mybir as mybir
from concourse.masks import make_identity

F32 = mybir.dt.float32
BF16 = mybir.dt.bfloat16
I32 = mybir.dt.int32
U32 = mybir.dt.uint32
U8 = mybir.dt.uint8
FP8X4 = mybir.dt.float8_e4m3fn_x4
ALU = mybir.AluOpType
IDENTITY = mybir.ActivationFunctionType.Identity
AXIS_X = mybir.AxisListType.X

P = 128
PACK = 4
QUADRANT = 32
IMAGES = 4
CHANNELS = P * PACK
PIXELS = 1024
ROW_TILES = CHANNELS // P
N_PASS = 512
HALVES = PIXELS // N_PASS
RESULTS = 2
EPS = 1e-5
RUN = 4
ROW_PAIRS = (slice(0, 2), slice(2, 4))
ROWS_ALONE = (slice(0, 1), slice(1, 2), slice(2, 3), slice(3, 4))
ALL_ROWS = slice(0, 4)
CHUNK = 64
WEAVE = 2
LEAD = 3
BOTH = slice(0, 2)
WITH_BIASES = slice(0, 4)
PASSES = RESULTS * ROW_TILES * HALVES
MOVE_BEHIND = 12

FLOPS = 2 * RESULTS * IMAGES * CHANNELS * CHANNELS * PIXELS


def tile_wb_pa_t_kernel(tc, x, Wc_words, Wc_scales, bc, W1_words, W1_scales, b1, out_0, out_1):
    nc = tc.nc
    words_in = (Wc_words, W1_words)
    scales_in = (Wc_scales, W1_scales)
    bias_in = (bc, b1)
    outs = (out_0, out_1)

    with ExitStack() as ctx:
        consts = ctx.enter_context(tc.tile_pool(name="consts", bufs=1))
        images = ctx.enter_context(tc.tile_pool(name="images", bufs=IMAGES))
        work = ctx.enter_context(tc.tile_pool(name="work", bufs=2))
        small = ctx.enter_context(tc.tile_pool(name="small", bufs=2))
        results = ctx.enter_context(tc.tile_pool(name="results", bufs=16))
        banks = ctx.enter_context(tc.psum_pool(name="banks", bufs=6))
        moves = ctx.enter_context(tc.psum_pool(name="moves", bufs=1))
        ctx.enter_context(tc.manual_schedule())

        bias4 = []
        for r in range(RESULTS):
            bias_r = consts.tile([P, PACK], BF16, name="bias4_%d" % r)
            nc.scalar.dma_start(out=bias_r[:], in_=bias_in[r].rearrange("(p j) -> p j", j=PACK))
            bias4.append(bias_r)

        warm = consts.tile([P, 2], F32)
        nc.gpsimd.memset(warm[:], 0.0)
        nc.scalar.activation(out=warm[:, 1:2], in_=warm[:, 0:1], func=IDENTITY)

        w_words = consts.tile([P, RESULTS, CHANNELS], U32, align_bytes=64)
        w_scales = consts.tile([P, RESULTS, CHANNELS], U8, align_bytes=64)
        nc.vector.memset(w_scales[:].bitcast(I32), 0)

        def load_image(b):
            raw = images.tile([P, PACK, PIXELS], BF16, name="raw")
            rows_of_p = x[b].rearrange("(p j) h w -> p j (h w)", j=PACK)
            for part_of in ROWS_ALONE if b == 0 else (ALL_ROWS,):
                nc.sync.dma_start(out=raw[:, part_of, :], in_=rows_of_p[:, part_of, :])
            return raw

        def load_scales(r):
            for q in range(P // QUADRANT):
                nc.sync.dma_start(
                    out=w_scales[QUADRANT * q : QUADRANT * q + PACK, r, :].bitcast(I32),
                    in_=scales_in[r][0, PACK * q : PACK * q + PACK, :].bitcast(I32),
                )

        def load_words(r):
            nc.sync.dma_start(
                out=w_words[:, r, :].bitcast(I32),
                in_=words_in[r][0].rearrange("p n t -> p (n t)").bitcast(I32),
            )

        raws = [load_image(0)]
        load_words(0)
        raws.append(load_image(1))
        load_scales(0)
        load_words(1)
        raws.append(load_image(2))
        load_scales(1)
        raws.append(load_image(3))

        ident = consts.tile([P, P], F32)
        make_identity(nc, ident[:])
        quad = consts.tile([P, ROW_TILES], F32)
        nc.vector.tensor_reduce(
            out=quad[:], in_=ident[:].rearrange("p (t l) -> p t l", l=QUADRANT), axis=AXIS_X, op=ALU.add
        )
        lane = consts.tile([P, QUADRANT], F32)
        nc.vector.tensor_reduce(
            out=lane[:], in_=ident[:].rearrange("p (t l) -> p l t", l=QUADRANT), axis=AXIS_X, op=ALU.add
        )
        pick = consts.tile([P, PACK], F32)
        nc.vector.tensor_reduce(
            out=pick[:], in_=ident[:].rearrange("p (l j) -> p j l", j=PACK), axis=AXIS_X, op=ALU.add
        )
        fold = consts.tile([P, QUADRANT, PACK], F32)
        nc.vector.tensor_copy(out=fold[:], in_=lane[:].unsqueeze(2).to_broadcast([P, QUADRANT, PACK]))
        quad_mean = consts.tile([P, ROW_TILES], F32)
        nc.vector.tensor_scalar_mul(out=quad_mean[:], in0=quad[:], scalar1=1.0 / PIXELS)

        def over_tiles(vec4):
            return vec4[:].unsqueeze(2).to_broadcast([P, PACK, ROW_TILES])

        def over_pack(mask):
            return mask[:].unsqueeze(1).to_broadcast([P, PACK, ROW_TILES])

        def n_of(some):
            return some.stop - some.start

        def move_to_rows(spread, moved, some):
            nc.tensor.matmul(
                out=moved[:, some, :, :].rearrange("p r j t -> p (r j t)"),
                lhsT=fold[:].rearrange("p l i -> p (l i)"),
                rhs=spread[:, some, :, :].rearrange("p r j t -> p (r j t)"),
                start=True,
                stop=True,
            )

        def mask_rows(masked, moved, some):
            nc.vector.tensor_tensor(
                out=masked[:, some, :, :],
                in0=moved[:, some, :, :],
                in1=pick[:].unsqueeze(1).unsqueeze(3).to_broadcast([P, n_of(some), PACK, ROW_TILES]),
                op=ALU.mult,
            )

        def take_rows(rows, masked, some):
            nc.vector.tensor_reduce(
                out=rows[:, some, :], in_=masked[:, some, :, :].rearrange("p r j t -> p r t j"), axis=AXIS_X, op=ALU.add
            )

        first_spread = consts.tile([P, 2 * RESULTS, PACK, ROW_TILES], F32)
        first_masked = consts.tile([P, 2 * RESULTS, PACK, ROW_TILES], F32)
        first_rows = consts.tile([P, 2 * RESULTS, ROW_TILES], F32)
        for r in range(RESULTS):
            nc.gpsimd.tensor_tensor(
                out=first_spread[:, RESULTS + r, :, :], in0=over_tiles(bias4[r]), in1=over_pack(quad), op=ALU.mult
            )
        bias_rows = first_rows[:, RESULTS:, :]
        ident_bf = consts.tile([P, P], BF16)
        make_identity(nc, ident_bf[:])
        averager = consts.tile([P, P], BF16)
        nc.gpsimd.tensor_scalar(
            out=averager[:], in0=ident_bf[:], scalar1=1.0 / PIXELS, scalar2=0.0, op0=ALU.mult, op1=ALU.add
        )

        def sum_steps(b):
            part = moves.tile([P, PACK, CHUNK], F32, name="part")
            n_chunks = PIXELS // CHUNK

            def step(i):
                nc.tensor.matmul(
                    out=part[:],
                    lhsT=averager[:],
                    rhs=raws[b][:, :, i * CHUNK : (i + 1) * CHUNK],
                    start=(i == 0),
                    stop=(i == n_chunks - 1),
                )

            return part, [(step, i) for i in range(n_chunks)]

        halves = consts.tile([P, PIXELS // 2], F32)
        go = consts.tile([P, IMAGES], F32)
        junk = consts.tile([P, PACK, PIXELS], BF16)

        def steps_of(b):
            raw = raws[b]
            img = {}

            def row_max(j):
                nc.vector.tensor_scalar(
                    out=junk[:, j, :],
                    in0=raw[:, j, :],
                    scalar1=1.0,
                    scalar2=None,
                    op0=ALU.mult,
                    op1=ALU.max,
                    accum_out=img["stat"][:, 1, j : j + 1],
                )

            def begin():
                img["stat"] = small.tile([P, RESULTS, PACK], F32, name="stat")
                img["grouped"] = work.tile([P, PIXELS, PACK], BF16, align_bytes=64, name="grouped")
                img["codes"] = work.tile([P, PIXELS], U32, align_bytes=64, name="codes")
                img["scales"] = work.tile([P, PIXELS], U8, align_bytes=64, name="scales")
                if b == 0:
                    img["spread"], img["masked"], img["den"] = first_spread, first_masked, first_rows
                else:
                    img["spread"] = small.tile([P, RESULTS, PACK, ROW_TILES], F32, name="spread")
                    img["masked"] = small.tile([P, RESULTS, PACK, ROW_TILES], F32, name="masked")
                    img["den"] = small.tile([P, RESULTS, ROW_TILES], F32, name="den")
                img["gain"] = small.tile([P, RESULTS, ROW_TILES], F32, name="gain")
                img["shift"] = small.tile([P, RESULTS, ROW_TILES], F32, name="shift")

            def sums_on_scalar():
                waste = consts.tile([P, PACK, PIXELS], BF16, name="waste")
                for j in range(PACK - 1):
                    nc.scalar.activation(
                        out=waste[:, j, :], in_=raw[:, j, :], func=IDENTITY, accum_out=img["stat"][:, 0, j : j + 1]
                    )

            def last_sum_on_vector():
                j = PACK - 1
                nc.vector.scalar_tensor_tensor(
                    out=halves[:],
                    in0=raw[:, j, : PIXELS // 2],
                    scalar=1.0,
                    in1=raw[:, j, PIXELS // 2 :],
                    op0=ALU.mult,
                    op1=ALU.add,
                    accum_out=img["stat"][:, 0, j : j + 1],
                )

            def take_means(part):
                nc.vector.tensor_reduce(out=img["stat"][:, 0, :], in_=part[:], axis=AXIS_X, op=ALU.add)

            def spread_both():
                groups = RESULTS * PACK
                nc.vector.scalar_tensor_tensor(
                    out=img["spread"][:].rearrange("p r j t -> p (r j) t"),
                    in0=img["stat"][:].rearrange("p r j -> p (r j)").unsqueeze(2).to_broadcast([P, groups, ROW_TILES]),
                    scalar=EPS,
                    in1=quad[:].unsqueeze(1).to_broadcast([P, groups, ROW_TILES]),
                    op0=ALU.add,
                    op1=ALU.mult,
                )

            def regroup(h):
                cols = slice(h * N_PASS, (h + 1) * N_PASS)
                nc.vector.tensor_copy(
                    out=img["grouped"][:, cols, :].rearrange("p (c i) j -> p c j i", i=RUN),
                    in_=raw[:, :, cols].rearrange("p j (c i) -> p c j i", i=RUN),
                )

            def regroup_on_scalar(h):
                cols = slice(h * N_PASS, (h + 1) * N_PASS)
                nc.scalar.copy(
                    out=img["grouped"][:, cols, :].rearrange("p (c i) j -> p c j i", i=RUN),
                    in_=raw[:, :, cols].rearrange("p j (c i) -> p c j i", i=RUN),
                )

            def signal_gpsimd():
                nc.vector.memset(go[:, b : b + 1], 1.0)

            def regroup_on_gpsimd(h):
                cols = slice(h * N_PASS, (h + 1) * N_PASS)
                nc.gpsimd.tensor_scalar(
                    out=img["grouped"][:, cols, :],
                    in0=raw[:, :, cols].rearrange("p j w -> p w j"),
                    scalar1=go[:, b : b + 1],
                    scalar2=0.0,
                    op0=ALU.mult,
                    op1=ALU.add,
                )

            def quantize(h):
                cols = slice(h * N_PASS, (h + 1) * N_PASS)
                nc.vector.quantize_mx(
                    out=img["codes"][:, cols].bitcast(FP8X4),
                    scales=img["scales"][:, cols],
                    in_=img["grouped"][:, cols, :].rearrange("p w j -> p (w j)"),
                )

            def spread_max():
                nc.vector.scalar_tensor_tensor(
                    out=img["spread"][:, 1, :, :],
                    in0=img["stat"][:, 1, :].unsqueeze(2).to_broadcast([P, PACK, ROW_TILES]),
                    scalar=EPS,
                    in1=over_pack(quad),
                    op0=ALU.add,
                    op1=ALU.mult,
                )

            def spread_sum():
                nc.vector.scalar_tensor_tensor(
                    out=img["spread"][:, 0, :, :],
                    in0=img["stat"][:, 0, :].unsqueeze(2).to_broadcast([P, PACK, ROW_TILES]),
                    scalar=PIXELS * EPS,
                    in1=over_pack(quad_mean),
                    op0=ALU.add,
                    op1=ALU.mult,
                )

            def move(some):
                img["moved"] = moves.tile([P, n_of(some), PACK, ROW_TILES], F32, name="moved")
                move_to_rows(img["spread"], img["moved"], some)

            def mask(some):
                mask_rows(img["masked"], img["moved"], some)

            def take(some):
                take_rows(img["den"], img["masked"], some)

            def invert(some):
                nc.vector.reciprocal(out=img["gain"][:, some, :], in_=img["den"][:, some, :])

            def scale_bias(some):
                nc.vector.tensor_mul(
                    out=img["shift"][:, some, :], in0=bias_rows, in1=img["gain"][:, some, :]
                )

            img["row_max"] = row_max
            img["begin"] = begin
            img["sums_on_scalar"] = sums_on_scalar
            img["last_sum_on_vector"] = last_sum_on_vector
            img["take_means"] = take_means
            img["spread_both"] = spread_both
            img["regroup"] = regroup
            img["regroup_on_scalar"] = regroup_on_scalar
            img["quantize"] = quantize
            img["signal_gpsimd"] = signal_gpsimd
            img["regroup_on_gpsimd"] = regroup_on_gpsimd
            img["spread_max"] = spread_max
            img["spread_sum"] = spread_sum
            img["move"] = move
            img["mask"] = mask
            img["take"] = take
            img["invert"] = invert
            img["scale_bias"] = scale_bias
            return img

        def one_pass(img, r, t, h):
            acc = banks.tile([P, N_PASS], F32, name="acc")
            cols = slice(h * N_PASS, (h + 1) * N_PASS)
            rows = slice(t * P, (t + 1) * P)
            nc.tensor.matmul_mx(
                out=acc[:],
                lhsT=w_words[:, r, rows].bitcast(FP8X4),
                lhsT_scale=w_scales[:, r, rows],
                rhs=img["codes"][:, cols].bitcast(FP8X4),
                rhs_scale=img["scales"][:, cols],
                start=True,
                stop=True,
            )
            return acc

        def empty(on_vector, img, acc, done, r, t, h):
            cols = slice(h * N_PASS, (h + 1) * N_PASS)
            if on_vector:
                nc.vector.tensor_scalar(
                    out=done[:, cols],
                    in0=acc[:],
                    scalar1=img["gain"][:, r, t : t + 1],
                    scalar2=img["shift"][:, r, t : t + 1],
                    op0=ALU.mult,
                    op1=ALU.add,
                )
            else:
                nc.scalar.activation(
                    out=done[:, cols],
                    in_=acc[:],
                    func=IDENTITY,
                    bias=img["shift"][:, r, t : t + 1],
                    scale=img["gain"][:, r, t : t + 1],
                )

        def store(b, r, t, done, h):
            rows_out = outs[r][b, t * P : (t + 1) * P].rearrange("c h w -> c (h w)")
            if h is None:
                nc.sync.dma_start(out=rows_out, in_=done[:])
            else:
                cols = slice(h * N_PASS, (h + 1) * N_PASS)
                nc.sync.dma_start(out=rows_out[:, cols], in_=done[:, cols])

        imgs = [steps_of(b) for b in range(IMAGES)]
        img = imgs[0]
        img["begin"]()
        img["sums_on_scalar"]()
        img["regroup_on_scalar"](1)
        for j in range(PACK):
            img["row_max"](j)
        img["last_sum_on_vector"]()
        img["spread_max"]()
        img["spread_sum"]()
        img["move"](WITH_BIASES)
        img["regroup"](0)
        img["mask"](WITH_BIASES)
        img["quantize"](0)
        img["take"](WITH_BIASES)
        img["invert"](BOTH)
        img["scale_bias"](BOTH)
        img["quantize"](1)

        plain_order = [(r, t, h) for r in range(RESULTS) for t in range(ROW_TILES) for h in range(HALVES)]
        for b in range(IMAGES):
            img = imgs[b]
            last = b == IMAGES - 1
            halves_leave = PASSES // 2 if b == 0 else 0
            order = plain_order
            if b == 0:
                order = [(0, t, h) for h in range(HALVES) for t in range(ROW_TILES)] + plain_order[PASSES // 2 :]
            dones = {}
            filled = {}

            def run(k):
                r, t, h = order[k]
                if (r, t) not in dones:
                    dones[(r, t)] = results.tile([P, PIXELS], F32, name="done")
                    filled[(r, t)] = 0
                return one_pass(img, r, t, h)

            def leave(k, on_vector, acc):
                r, t, h = order[k]
                empty(on_vector, img, acc, dones[(r, t)], r, t, h)
                filled[(r, t)] += 1
                if k < halves_leave:
                    store(b, r, t, dones[(r, t)], h)
                elif filled[(r, t)] == HALVES:
                    store(b, r, t, dones[(r, t)], None)

            if last:
                for k in range(PASSES):
                    leave(k, k % 2 == 1, run(k))
                continue

            nxt = imgs[b + 1]
            part, woven = sum_steps(b + 1)
            for k in range(PASSES // 2):
                acc = run(k)
                if k + 1 >= LEAD:
                    for step, i in woven[:WEAVE]:
                        step(i)
                    woven = woven[WEAVE:]
                leave(k, False, acc)
            nxt["begin"]()
            nxt["regroup"](0)
            nxt["signal_gpsimd"]()
            nxt["regroup_on_gpsimd"](1)
            for j in range(PACK):
                nxt["row_max"](j)
            mine = (PASSES - 1,) if b == 0 else (PASSES - 2, PASSES - 1)
            accs = {}
            for k in range(PASSES // 2, PASSES):
                accs[k] = run(k)
                for step, i in woven[:WEAVE]:
                    step(i)
                woven = woven[WEAVE:]
                if k not in mine:
                    leave(k, False, accs[k])
                if k == MOVE_BEHIND:
                    assert not woven
                    nxt["take_means"](part)
                    nxt["quantize"](0)
                    nxt["spread_both"]()
                    nxt["move"](BOTH)
            nxt["quantize"](1)
            nxt["mask"](BOTH)
            if len(mine) == 2:
                leave(mine[0], True, accs[mine[0]])
            nxt["take"](BOTH)
            leave(PASSES - 1, True, accs[PASSES - 1])
            nxt["invert"](BOTH)
            nxt["scale_bias"](BOTH)
